import numpy as np
import ml_dtypes


def mxq(x, axis, fmt="e4m3"):
    dtype, down = {"e4m3": (ml_dtypes.float8_e4m3fn, 7), "e5m2": (ml_dtypes.float8_e5m2, 14)}[fmt]
    v = np.moveaxis(np.asarray(x, np.float32).astype(ml_dtypes.bfloat16).astype(np.float64), axis, -1)
    blocks = v.reshape(v.shape[:-1] + (-1, 32))
    amax = np.abs(blocks).max(-1, keepdims=True)
    byte = np.maximum(np.where(amax > 0, np.frexp(amax)[1] - 1 + 127, 0) - down, 1)
    scale = np.exp2(byte - 127.0)
    codes = (blocks / scale).astype(np.float32).astype(dtype).astype(np.float64)
    return np.moveaxis((codes * scale).reshape(v.shape), -1, axis)


WIDE = False


def mx_kscale(k):
    if not WIDE:
        return np.ones(k)
    levels = np.array([10, -10, 5, -5, 0])
    a = np.random.permutation(np.resize(levels, k // 512 * 4)).reshape(k // 512, 4)
    idx = np.arange(k)
    return np.exp2(a[idx // 512, idx % 128 // 32])


BF16 = ml_dtypes.bfloat16


def bf(x):
    return np.asarray(x, np.float32).astype(BF16)


def f64(x):
    return np.asarray(x).astype(np.float64)


E2M1 = np.array([0.0, 0.5, 1.0, 1.5, 2.0, 3.0, 4.0, 6.0, -0.0, -0.5, -1.0, -1.5, -2.0, -3.0, -4.0, -6.0])


def pack_weight(w, fmt):
    k, n = w.shape
    w = f64(bf(w)).reshape(k // 32, 32, n)
    amax = np.abs(w).max(1)
    if fmt == "e4m3":
        byte = np.frexp(amax)[1] - 1 + 127 - 7
    else:
        mant, ex = np.frexp(amax / 6.0)
        byte = np.where(mant > 0.5, ex, ex - 1) + 127
    byte = np.clip(np.where(amax > 0, byte, 1), 1, 254)
    scaled = (w * np.exp2(127.0 - byte)[:, None, :]).reshape(k, n).astype(np.float32)
    by_word = np.ascontiguousarray(scaled.reshape(k // 512, 128, 4, n).transpose(0, 1, 3, 2))
    if fmt == "e4m3":
        words = by_word.astype(ml_dtypes.float8_e4m3fn).view(np.uint8)
    else:
        c = by_word.astype(ml_dtypes.float4_e2m1fn).view(np.uint8) & 0xF
        words = c[..., 0::2] | (c[..., 1::2] << 4)
    return np.ascontiguousarray(words), np.ascontiguousarray(byte.astype(np.uint8).reshape(k // 512, 16, n))


def unpack_weight(words, scales, fmt):
    g, p, n, _ = words.shape
    if fmt == "e4m3":
        vals = np.ascontiguousarray(words).view(ml_dtypes.float8_e4m3fn).astype(np.float64)
    else:
        nib = np.empty((g, p, n, 4), np.uint8)
        nib[..., 0::2] = words & 0xF
        nib[..., 1::2] = words >> 4
        vals = E2M1[nib]
    vals = vals * np.repeat(np.exp2(scales.astype(np.float64) - 127.0), 8, axis=1)[..., None]
    return vals.transpose(0, 1, 3, 2).reshape(g * 512, n)


B, D_IN, D_H = 256, 16384, 1024


def sigmoid(v):
    return 1.0 / (1.0 + np.exp(-v))


def setup_inputs():
    s, t = mx_kscale(D_IN), mx_kscale(D_H)
    fg = np.exp(0.75 * np.random.standard_normal((B, D_H)))
    ig = np.exp(0.75 * np.random.standard_normal((B, D_H)))
    c = fg * np.random.standard_normal((B, D_H)) + ig * np.tanh(0.75 * np.random.standard_normal((B, D_H)))
    n = fg * np.random.uniform(size=(B, D_H)) + ig
    x = bf(np.random.standard_normal((B, D_IN)) * s)
    h_prev = bf(np.random.standard_normal((B, D_H)) * t)
    W_o_words, W_o_scales = pack_weight(np.random.standard_normal((D_IN, D_H)) * 0.5 / np.sqrt(D_IN) / s[:, None], "e4m3")
    b_o = bf(np.random.standard_normal(D_H) * 0.3)
    U_o_words, U_o_scales = pack_weight(np.random.standard_normal((D_H, D_H)) * 0.5 / np.sqrt(D_H) / t[:, None], "e4m3")
    return {"x": x,
            "h_prev": h_prev,
            "c": bf(c),
            "n": bf(n),
            "W_o_words": W_o_words,
            "W_o_scales": W_o_scales,
            "b_o": b_o,
            "U_o_words": U_o_words,
            "U_o_scales": U_o_scales}


def reference(x, h_prev, c, n, W_o_words, W_o_scales, b_o, U_o_words, U_o_scales):
    o = sigmoid((mxq(f64(x), 1, "e4m3") @ unpack_weight(W_o_words, W_o_scales, "e4m3")) + f64(b_o) + (mxq(f64(h_prev), 1, "e4m3") @ unpack_weight(U_o_words, U_o_scales, "e4m3")))
    return o * (f64(c) / (f64(n) + 1e-6))

@@ -1,0 +1,236 @@
+from contextlib import ExitStack
+
+import concourse.mybir as mybir
+from concourse.masks import make_identity
+
+F32 = mybir.dt.float32
+BF16 = mybir.dt.bfloat16
+I32 = mybir.dt.int32
+U32 = mybir.dt.uint32
+U8 = mybir.dt.uint8
+FP8X4 = mybir.dt.float8_e4m3fn_x4
+ADD = mybir.AluOpType.add
+MULT = mybir.AluOpType.mult
+SIGMOID = mybir.ActivationFunctionType.Sigmoid
+
+P = 128
+K_PASS = 512
+PAIRS = K_PASS // 2
+BATCH = 256
+M_TILES = BATCH // P
+D_IN = 16384
+D_H = 1024
+N_TILE = 512
+N_TILES = D_H // N_TILE
+ROUND = 4
+X_ROUNDS = D_IN // (ROUND * K_PASS)
+ROUNDS = 1 + X_ROUNDS
+W_LOAD = 2
+SCALE_ROWS = K_PASS // 32
+RATIO_COLS = M_TILES * D_H // X_ROUNDS
+AHEAD = 3
+
+FLOPS = 2 * BATCH * (D_IN + D_H) * D_H
+
+
+def groups_in(r):
+    return D_H // K_PASS if r == 0 else ROUND
+
+
+def tile_slstmcell_pb_k_kernel(
+    tc, x, h_prev, c, n, W_o_words, W_o_scales, b_o, U_o_words, U_o_scales, out
+):
+    nc = tc.nc
+
+    x_rows = x.rearrange("(m p) k -> p m k", p=P)
+    h_rows = h_prev.rearrange("(m p) k -> p m k", p=P)
+    c_rows = c.rearrange("(m p) j -> p m j", p=P)
+    n_rows = n.rearrange("(m p) j -> p m j", p=P)
+    w_words = W_o_words.rearrange("g p j t -> p g (j t)").bitcast(I32)
+    u_words = U_o_words.rearrange("g p j t -> p g (j t)").bitcast(I32)
+    w_scale_rows = W_o_scales.bitcast(I32).rearrange("(r i) q w -> q i r w", i=ROUND)
+    u_scale_rows = U_o_scales.bitcast(I32)
+
+    with ExitStack() as ctx:
+        keep = ctx.enter_context(tc.tile_pool(name="keep", bufs=1))
+        act_pool = ctx.enter_context(tc.tile_pool(name="act", bufs=AHEAD + 1))
+        w_pool = ctx.enter_context(tc.tile_pool(name="w", bufs=(AHEAD + 1) * ROUND // W_LOAD))
+        grouped_pool = ctx.enter_context(tc.tile_pool(name="grouped", bufs=4))
+        code_pool = ctx.enter_context(tc.tile_pool(name="codes", bufs=3))
+        work = ctx.enter_context(tc.tile_pool(name="work", bufs=2))
+        readout = ctx.enter_context(tc.tile_pool(name="readout", bufs=M_TILES * N_TILES))
+        sums = ctx.enter_context(tc.psum_pool(name="sums", bufs=1))
+        banks = ctx.enter_context(tc.psum_pool(name="banks", bufs=ROUND))
+        ctx.enter_context(tc.manual_schedule())
+
+        planes = keep.tile([P, ROUNDS, D_H], U8, align_bytes=64)
+        planes_i32 = planes[:].bitcast(I32)
+        nc.vector.memset(planes_i32, 0)
+        bias_row = keep.tile([P, D_H], BF16)
+        nc.vector.memset(bias_row[:].bitcast(I32), 0)
+        ones = keep.tile([P, P], BF16)
+        nc.vector.memset(ones[:], 1.0)
+        table_in = keep.tile([P, 1], F32)
+        nc.vector.memset(table_in[:], 0.0)
+        ident = keep.tile([P, P], F32)
+        make_identity(nc, ident[:])
+        table_out = keep.tile([P, 1], F32)
+        nc.scalar.activation(out=table_out[:], in_=table_in[:], func=SIGMOID)
+
+        acts = {}
+        weights = {}
+
+        def load_activations(r):
+            cols = groups_in(r) * K_PASS
+            act = act_pool.tile([P, M_TILES, cols], BF16, name="act")
+            if r == 0:
+                nc.sync.dma_start(out=act[:], in_=h_rows)
+            else:
+                nc.sync.dma_start(out=act[:], in_=x_rows[:, :, (r - 1) * cols : r * cols])
+            acts[r] = act
+
+        def load_weights(r):
+            for first in range(0, groups_in(r), W_LOAD):
+                words = w_pool.tile([P, W_LOAD, D_H], U32, name="words", align_bytes=64)
+                if r == 0:
+                    src = u_words
+                else:
+                    g = (r - 1) * ROUND + first
+                    src = w_words[:, g : g + W_LOAD, :]
+                nc.sync.dma_start(out=words[:].bitcast(I32), in_=src)
+                weights[(r, first)] = words
+
+        def load_scale_rows():
+            for quad in range(SCALE_ROWS // 4):
+                nc.sync.dma_start(
+                    out=planes_i32[32 * quad : 32 * quad + 8, 0, :],
+                    in_=u_scale_rows[:, 4 * quad : 4 * quad + 4, :],
+                )
+            for q in range(SCALE_ROWS):
+                first = 32 * (q // 4) + q % 4
+                nc.sync.dma_start(
+                    out=planes_i32[first : first + 4 * ROUND : 4, 1:ROUNDS, :],
+                    in_=w_scale_rows[q],
+                )
+
+        load_activations(0)
+        load_activations(1)
+        nc.sync.dma_start(out=bias_row[0:1, :], in_=b_o.unsqueeze(0))
+        load_scale_rows()
+        load_weights(0)
+        load_activations(2)
+        load_weights(1)
+        c_sb = keep.tile([P, M_TILES * D_H], BF16)
+        n_sb = keep.tile([P, M_TILES * D_H], BF16)
+        nc.sync.dma_start(out=n_sb[:].rearrange("p (m j) -> p m j", m=M_TILES), in_=n_rows)
+        nc.sync.dma_start(out=c_sb[:].rearrange("p (m j) -> p m j", m=M_TILES), in_=c_rows)
+        load_activations(3)
+        load_weights(2)
+
+        acc = {}
+        for m in range(M_TILES):
+            for j in range(N_TILES):
+                acc[(m, j)] = sums.tile([P, N_TILE], F32, name="acc%d%d" % (m, j))
+        bias_all = keep.tile([P, D_H], F32)
+        ratio = keep.tile([P, M_TILES * D_H], F32)
+        codes = {}
+
+        def transpose_and_quantise(r):
+            x_words = code_pool.tile([P, ROUND, BATCH], U32, name="x_words", align_bytes=64)
+            x_planes = code_pool.tile([P, ROUND, BATCH], U8, name="x_planes", align_bytes=64)
+            codes[r] = (x_words, x_planes)
+            for g in range(groups_in(r)):
+                bank = banks.tile([P, 2, BATCH], F32, name="bank")
+                for u in range(2):
+                    for m in range(M_TILES):
+                        pairs = acts[r][:, m, :].bitcast(F32)
+                        nc.tensor.transpose(
+                            bank[:, u, m * P : (m + 1) * P],
+                            pairs[:, g * PAIRS + u : (g + 1) * PAIRS : 2],
+                            ident[:],
+                        )
+                grouped = grouped_pool.tile([P, BATCH * 4], BF16, name="grouped", align_bytes=64)
+                nc.scalar.copy(
+                    out=grouped[:].bitcast(F32).rearrange("p (b u) -> p b u", u=2),
+                    in_=bank[:].rearrange("p u b -> p b u"),
+                )
+                nc.vector.quantize_mx(
+                    out=x_words[:, g, :].bitcast(FP8X4), scales=x_planes[:, g, :], in_=grouped[:]
+                )
+
+        def ratio_block(i):
+            cols = slice(i * RATIO_COLS, (i + 1) * RATIO_COLS)
+            den = work.tile([P, RATIO_COLS], F32, name="den")
+            nc.vector.tensor_scalar(
+                out=den[:], in0=n_sb[:, cols], scalar1=1e-6, scalar2=None, op0=ADD
+            )
+            inv = work.tile([P, RATIO_COLS], F32, name="inv")
+            nc.vector.reciprocal(out=inv[:], in_=den[:])
+            nc.vector.tensor_tensor(out=ratio[:, cols], in0=inv[:], in1=c_sb[:, cols], op=MULT)
+
+        def spread_bias():
+            for j in range(N_TILES):
+                cols = slice(j * N_TILE, (j + 1) * N_TILE)
+                bank = banks.tile([P, N_TILE], F32, name="bank")
+                nc.tensor.matmul(
+                    out=bank[:], lhsT=ones[:], rhs=bias_row[:, cols], start=True, stop=True
+                )
+                nc.scalar.copy(out=bias_all[:, cols], in_=bank[:])
+
+        def passes(r):
+            x_words, x_planes = codes[r]
+            for g in range(groups_in(r)):
+                words = weights[(r, g - g % W_LOAD)]
+                for m in range(M_TILES):
+                    rows = slice(m * P, (m + 1) * P)
+                    for j in range(N_TILES):
+                        cols = slice(j * N_TILE, (j + 1) * N_TILE)
+                        nc.tensor.matmul_mx(
+                            out=acc[(m, j)][:],
+                            lhsT=x_words[:, g, rows].bitcast(FP8X4),
+                            lhsT_scale=x_planes[:, g, rows],
+                            rhs=words[:, g % W_LOAD, cols].bitcast(FP8X4),
+                            rhs_scale=planes[4 * g : P, r, cols],
+                            start=(r == 0 and g == 0),
+                            stop=(r == ROUNDS - 1 and g == groups_in(r) - 1),
+                        )
+
+        transpose_and_quantise(0)
+        for r in range(ROUNDS):
+            if r + AHEAD + 1 < ROUNDS:
+                load_activations(r + AHEAD + 1)
+            if r + AHEAD < ROUNDS:
+                load_weights(r + AHEAD)
+            if r + 1 < ROUNDS:
+                transpose_and_quantise(r + 1)
+                ratio_block(r)
+            if r == 0:
+                spread_bias()
+            passes(r)
+
+        order = [(m, j) for m in range(M_TILES) for j in range(N_TILES)]
+        gates = {}
+        for i in range(len(order) + 1):
+            if i < len(order):
+                m, j = order[i]
+                pre = readout.tile([P, N_TILE], F32, name="pre")
+                nc.vector.tensor_tensor(
+                    out=pre[:],
+                    in0=acc[(m, j)][:],
+                    in1=bias_all[:, j * N_TILE : (j + 1) * N_TILE],
+                    op=ADD,
+                )
+                gates[i] = readout.tile([P, N_TILE], F32, name="gate")
+                nc.scalar.activation(out=gates[i][:], in_=pre[:], func=SIGMOID)
+            if i > 0:
+                m, j = order[i - 1]
+                res = readout.tile([P, N_TILE], F32, name="res")
+                nc.vector.tensor_tensor(
+                    out=res[:],
+                    in0=gates[i - 1][:],
+                    in1=ratio[:, m * D_H + j * N_TILE : m * D_H + (j + 1) * N_TILE],
+                    op=MULT,
+                )
+                nc.sync.dma_start(
+                    out=out[m * P : (m + 1) * P, j * N_TILE : (j + 1) * N_TILE], in_=res[:]
+                )

@@ -15,7 +15,6 @@ SIGMOID = mybir.ActivationFunctionType.Sigmoid
 
 P = 128
 K_PASS = 512
-PAIRS = K_PASS // 2
 BATCH = 256
 M_TILES = BATCH // P
 D_IN = 16384
@@ -53,8 +52,9 @@ def tile_slstmcell_pb_k_kernel(
 
     with ExitStack() as ctx:
         keep = ctx.enter_context(tc.tile_pool(name="keep", bufs=1))
-        act_pool = ctx.enter_context(tc.tile_pool(name="act", bufs=AHEAD + 1))
+        act_pool = ctx.enter_context(tc.tile_pool(name="act", bufs=AHEAD + 2))
         w_pool = ctx.enter_context(tc.tile_pool(name="w", bufs=(AHEAD + 1) * ROUND // W_LOAD))
+        sorted_pool = ctx.enter_context(tc.tile_pool(name="sorted", bufs=2))
         grouped_pool = ctx.enter_context(tc.tile_pool(name="grouped", bufs=4))
         code_pool = ctx.enter_context(tc.tile_pool(name="codes", bufs=3))
         work = ctx.enter_context(tc.tile_pool(name="work", bufs=2))
@@ -117,14 +117,15 @@ def tile_slstmcell_pb_k_kernel(
         load_activations(1)
         nc.sync.dma_start(out=bias_row[0:1, :], in_=b_o.unsqueeze(0))
         load_scale_rows()
-        load_weights(0)
         load_activations(2)
+        load_weights(0)
+        load_activations(3)
         load_weights(1)
         c_sb = keep.tile([P, M_TILES * D_H], BF16)
         n_sb = keep.tile([P, M_TILES * D_H], BF16)
         nc.sync.dma_start(out=n_sb[:].rearrange("p (m j) -> p m j", m=M_TILES), in_=n_rows)
         nc.sync.dma_start(out=c_sb[:].rearrange("p (m j) -> p m j", m=M_TILES), in_=c_rows)
-        load_activations(3)
+        load_activations(4)
         load_weights(2)
 
         acc = {}
@@ -134,6 +135,16 @@ def tile_slstmcell_pb_k_kernel(
         bias_all = keep.tile([P, D_H], F32)
         ratio = keep.tile([P, M_TILES * D_H], F32)
         codes = {}
+        sorted_pairs = {}
+
+        def sort_pairs(r):
+            pairs = sorted_pool.tile([P, M_TILES, ROUND, 2, P], F32, name="pairs")
+            for m in range(M_TILES):
+                nc.scalar.copy(
+                    out=pairs[:, m, 0 : groups_in(r), :, :],
+                    in_=acts[r][:, m, :].bitcast(F32).rearrange("p (g q u) -> p g u q", q=P, u=2),
+                )
+            sorted_pairs[r] = pairs
 
         def transpose_and_quantise(r):
             x_words = code_pool.tile([P, ROUND, BATCH], U32, name="x_words", align_bytes=64)
@@ -143,11 +154,8 @@ def tile_slstmcell_pb_k_kernel(
                 bank = banks.tile([P, 2, BATCH], F32, name="bank")
                 for u in range(2):
                     for m in range(M_TILES):
-                        pairs = acts[r][:, m, :].bitcast(F32)
                         nc.tensor.transpose(
-                            bank[:, u, m * P : (m + 1) * P],
-                            pairs[:, g * PAIRS + u : (g + 1) * PAIRS : 2],
-                            ident[:],
+                            bank[:, u, m * P : (m + 1) * P], sorted_pairs[r][:, m, g, u, :], ident[:]
                         )
                 grouped = grouped_pool.tile([P, BATCH * 4], BF16, name="grouped", align_bytes=64)
                 nc.scalar.copy(
@@ -195,15 +203,19 @@ def tile_slstmcell_pb_k_kernel(
                             stop=(r == ROUNDS - 1 and g == groups_in(r) - 1),
                         )
 
+        sort_pairs(0)
+        sort_pairs(1)
         transpose_and_quantise(0)
         for r in range(ROUNDS):
-            if r + AHEAD + 1 < ROUNDS:
-                load_activations(r + AHEAD + 1)
+            if r + AHEAD + 2 < ROUNDS:
+                load_activations(r + AHEAD + 2)
             if r + AHEAD < ROUNDS:
                 load_weights(r + AHEAD)
             if r + 1 < ROUNDS:
                 transpose_and_quantise(r + 1)
                 ratio_block(r)
+            if r + 2 < ROUNDS:
+                sort_pairs(r + 2)
             if r == 0:
                 spread_bias()
             passes(r)

@@ -36,15 +36,23 @@ def groups_in(r):
     return D_H // K_PASS if r == 0 else ROUND
 
 
+def weight_blocks(r):
+    if r < ROUNDS - 1:
+        return [(g, W_LOAD, 0, N_TILES) for g in range(0, groups_in(r), W_LOAD)]
+    early = [(0, ROUND, j, 1) for j in range(N_TILES - 1)]
+    return early + [(g, W_LOAD, N_TILES - 1, 1) for g in range(0, ROUND, W_LOAD)]
+
+
 def tile_slstmcell_pb_k_kernel(
     tc, x, h_prev, c, n, W_o_words, W_o_scales, b_o, U_o_words, U_o_scales, out
 ):
     nc = tc.nc
 
-    x_rows = x.rearrange("(m p) k -> p m k", p=P)
-    h_rows = h_prev.rearrange("(m p) k -> p m k", p=P)
-    c_rows = c.rearrange("(m p) j -> p m j", p=P)
-    n_rows = n.rearrange("(m p) j -> p m j", p=P)
+    x_rows = x.rearrange("(p m) k -> p m k", m=M_TILES)
+    h_rows = h_prev.rearrange("(p m) k -> p m k", m=M_TILES)
+    c_rows = c.rearrange("(p m) j -> p (m j)", m=M_TILES)
+    n_rows = n.rearrange("(p m) j -> p (m j)", m=M_TILES)
+    out_rows = out.rearrange("(p m) j -> p m j", m=M_TILES)
     w_words = W_o_words.rearrange("g p j t -> p g (j t)").bitcast(I32)
     u_words = U_o_words.rearrange("g p j t -> p g (j t)").bitcast(I32)
     w_scale_rows = W_o_scales.bitcast(I32).rearrange("(r i) q w -> q i r w", i=ROUND)
@@ -53,7 +61,7 @@ def tile_slstmcell_pb_k_kernel(
     with ExitStack() as ctx:
         keep = ctx.enter_context(tc.tile_pool(name="keep", bufs=1))
         act_pool = ctx.enter_context(tc.tile_pool(name="act", bufs=AHEAD + 2))
-        w_pool = ctx.enter_context(tc.tile_pool(name="w", bufs=(AHEAD + 1) * ROUND // W_LOAD))
+        w_pool = ctx.enter_context(tc.tile_pool(name="w", bufs=(AHEAD + 1) * ROUND // W_LOAD + 1))
         sorted_pool = ctx.enter_context(tc.tile_pool(name="sorted", bufs=2))
         grouped_pool = ctx.enter_context(tc.tile_pool(name="grouped", bufs=4))
         code_pool = ctx.enter_context(tc.tile_pool(name="codes", bufs=3))
@@ -90,15 +98,17 @@ def tile_slstmcell_pb_k_kernel(
             acts[r] = act
 
         def load_weights(r):
-            for first in range(0, groups_in(r), W_LOAD):
-                words = w_pool.tile([P, W_LOAD, D_H], U32, name="words", align_bytes=64)
-                if r == 0:
-                    src = u_words
-                else:
-                    g = (r - 1) * ROUND + first
-                    src = w_words[:, g : g + W_LOAD, :]
-                nc.sync.dma_start(out=words[:].bitcast(I32), in_=src)
-                weights[(r, first)] = words
+            src = u_words if r == 0 else w_words[:, (r - 1) * ROUND : r * ROUND, :]
+            for block in weight_blocks(r):
+                g0, n_groups, j0, n_tiles = block
+                words = w_pool.tile(
+                    [P, n_groups, n_tiles * N_TILE], U32, name="words", align_bytes=64
+                )
+                nc.sync.dma_start(
+                    out=words[:].bitcast(I32),
+                    in_=src[:, g0 : g0 + n_groups, j0 * N_TILE : (j0 + n_tiles) * N_TILE],
+                )
+                weights[(r, block)] = words
 
         def load_scale_rows():
             for quad in range(SCALE_ROWS // 4):
@@ -123,8 +133,8 @@ def tile_slstmcell_pb_k_kernel(
         load_weights(1)
         c_sb = keep.tile([P, M_TILES * D_H], BF16)
         n_sb = keep.tile([P, M_TILES * D_H], BF16)
-        nc.sync.dma_start(out=n_sb[:].rearrange("p (m j) -> p m j", m=M_TILES), in_=n_rows)
-        nc.sync.dma_start(out=c_sb[:].rearrange("p (m j) -> p m j", m=M_TILES), in_=c_rows)
+        nc.sync.dma_start(out=n_sb[:], in_=n_rows)
+        nc.sync.dma_start(out=c_sb[:], in_=c_rows)
         load_activations(4)
         load_weights(2)
 
@@ -185,23 +195,48 @@ def tile_slstmcell_pb_k_kernel(
                 )
                 nc.scalar.copy(out=bias_all[:, cols], in_=bank[:])
 
-        def passes(r):
+        def passes(r, block):
             x_words, x_planes = codes[r]
-            for g in range(groups_in(r)):
-                words = weights[(r, g - g % W_LOAD)]
-                for m in range(M_TILES):
-                    rows = slice(m * P, (m + 1) * P)
-                    for j in range(N_TILES):
-                        cols = slice(j * N_TILE, (j + 1) * N_TILE)
+            g0, n_groups, j0, n_tiles = block
+            words = weights[(r, block)]
+            for m in range(M_TILES):
+                rows = slice(m * P, (m + 1) * P)
+                for g in range(g0, g0 + n_groups):
+                    for j in range(j0, j0 + n_tiles):
                         nc.tensor.matmul_mx(
                             out=acc[(m, j)][:],
                             lhsT=x_words[:, g, rows].bitcast(FP8X4),
                             lhsT_scale=x_planes[:, g, rows],
-                            rhs=words[:, g % W_LOAD, cols].bitcast(FP8X4),
-                            rhs_scale=planes[4 * g : P, r, cols],
+                            rhs=words[:, g - g0, (j - j0) * N_TILE : (j - j0 + 1) * N_TILE].bitcast(
+                                FP8X4
+                            ),
+                            rhs_scale=planes[4 * g : P, r, j * N_TILE : (j + 1) * N_TILE],
                             start=(r == 0 and g == 0),
-                            stop=(r == ROUNDS - 1 and g == groups_in(r) - 1),
+                            stop=(r == ROUNDS - 1 and g == ROUND - 1),
                         )
+
+        def read_out(j):
+            gates = []
+            for m in range(M_TILES):
+                pre = readout.tile([P, N_TILE], F32, name="pre")
+                nc.vector.tensor_tensor(
+                    out=pre[:],
+                    in0=acc[(m, j)][:],
+                    in1=bias_all[:, j * N_TILE : (j + 1) * N_TILE],
+                    op=ADD,
+                )
+                gate = readout.tile([P, N_TILE], F32, name="gate")
+                nc.scalar.activation(out=gate[:], in_=pre[:], func=SIGMOID)
+                gates.append(gate)
+            for m in range(M_TILES):
+                res = readout.tile([P, N_TILE], F32, name="res")
+                nc.vector.tensor_tensor(
+                    out=res[:],
+                    in0=gates[m][:],
+                    in1=ratio[:, m * D_H + j * N_TILE : m * D_H + (j + 1) * N_TILE],
+                    op=MULT,
+                )
+                nc.sync.dma_start(out=out_rows[:, m, j * N_TILE : (j + 1) * N_TILE], in_=res[:])
 
         sort_pairs(0)
         sort_pairs(1)
@@ -218,31 +253,8 @@ def tile_slstmcell_pb_k_kernel(
                 sort_pairs(r + 2)
             if r == 0:
                 spread_bias()
-            passes(r)
-
-        order = [(m, j) for m in range(M_TILES) for j in range(N_TILES)]
-        gates = {}
-        for i in range(len(order) + 1):
-            if i < len(order):
-                m, j = order[i]
-                pre = readout.tile([P, N_TILE], F32, name="pre")
-                nc.vector.tensor_tensor(
-                    out=pre[:],
-                    in0=acc[(m, j)][:],
-                    in1=bias_all[:, j * N_TILE : (j + 1) * N_TILE],
-                    op=ADD,
-                )
-                gates[i] = readout.tile([P, N_TILE], F32, name="gate")
-                nc.scalar.activation(out=gates[i][:], in_=pre[:], func=SIGMOID)
-            if i > 0:
-                m, j = order[i - 1]
-                res = readout.tile([P, N_TILE], F32, name="res")
-                nc.vector.tensor_tensor(
-                    out=res[:],
-                    in0=gates[i - 1][:],
-                    in1=ratio[:, m * D_H + j * N_TILE : m * D_H + (j + 1) * N_TILE],
-                    op=MULT,
-                )
-                nc.sync.dma_start(
-                    out=out[m * P : (m + 1) * P, j * N_TILE : (j + 1) * N_TILE], in_=res[:]
-                )
+            for block in weight_blocks(r):
+                passes(r, block)
+                g0, n_groups, j0, n_tiles = block
+                if r == ROUNDS - 1 and g0 + n_groups == ROUND:
+                    read_out(j0)

@@ -87,6 +87,7 @@ def tile_slstmcell_pb_k_kernel(
 
         acts = {}
         weights = {}
+        c_sb = keep.tile([P, M_TILES * D_H], BF16)
 
         def load_activations(r):
             cols = groups_in(r) * K_PASS
@@ -109,6 +110,8 @@ def tile_slstmcell_pb_k_kernel(
                     in_=src[:, g0 : g0 + n_groups, j0 * N_TILE : (j0 + n_tiles) * N_TILE],
                 )
                 weights[(r, block)] = words
+                if r == ROUNDS - 2 and block == weight_blocks(r)[0]:
+                    nc.sync.dma_start(out=c_sb[:], in_=c_rows)
 
         def load_scale_rows():
             for quad in range(SCALE_ROWS // 4):
@@ -131,10 +134,8 @@ def tile_slstmcell_pb_k_kernel(
         load_weights(0)
         load_activations(3)
         load_weights(1)
-        c_sb = keep.tile([P, M_TILES * D_H], BF16)
         n_sb = keep.tile([P, M_TILES * D_H], BF16)
         nc.sync.dma_start(out=n_sb[:], in_=n_rows)
-        nc.sync.dma_start(out=c_sb[:], in_=c_rows)
         load_activations(4)
         load_weights(2)
 
@@ -143,6 +144,7 @@ def tile_slstmcell_pb_k_kernel(
             for j in range(N_TILES):
                 acc[(m, j)] = sums.tile([P, N_TILE], F32, name="acc%d%d" % (m, j))
         bias_all = keep.tile([P, D_H], F32)
+        inv_all = keep.tile([P, M_TILES * D_H], F32)
         ratio = keep.tile([P, M_TILES * D_H], F32)
         codes = {}
         sorted_pairs = {}
@@ -176,15 +178,21 @@ def tile_slstmcell_pb_k_kernel(
                     out=x_words[:, g, :].bitcast(FP8X4), scales=x_planes[:, g, :], in_=grouped[:]
                 )
 
-        def ratio_block(i):
+        def inverse_block(i):
             cols = slice(i * RATIO_COLS, (i + 1) * RATIO_COLS)
             den = work.tile([P, RATIO_COLS], F32, name="den")
             nc.vector.tensor_scalar(
                 out=den[:], in0=n_sb[:, cols], scalar1=1e-6, scalar2=None, op0=ADD
             )
-            inv = work.tile([P, RATIO_COLS], F32, name="inv")
-            nc.vector.reciprocal(out=inv[:], in_=den[:])
-            nc.vector.tensor_tensor(out=ratio[:, cols], in0=inv[:], in1=c_sb[:, cols], op=MULT)
+            nc.vector.reciprocal(out=inv_all[:, cols], in_=den[:])
+
+        def ratios():
+            for j in range(N_TILES):
+                for m in range(M_TILES):
+                    cols = slice(m * D_H + j * N_TILE, m * D_H + (j + 1) * N_TILE)
+                    nc.vector.tensor_tensor(
+                        out=ratio[:, cols], in0=inv_all[:, cols], in1=c_sb[:, cols], op=MULT
+                    )
 
         def spread_bias():
             for j in range(N_TILES):
@@ -248,7 +256,9 @@ def tile_slstmcell_pb_k_kernel(
                 load_weights(r + AHEAD)
             if r + 1 < ROUNDS:
                 transpose_and_quantise(r + 1)
-                ratio_block(r)
+                inverse_block(r)
+            if r == ROUNDS - 2:
+                ratios()
             if r + 2 < ROUNDS:
                 sort_pairs(r + 2)
             if r == 0:

from contextlib import ExitStack

import concourse.mybir as mybir
from concourse.masks import make_identity

F32 = mybir.dt.float32
BF16 = mybir.dt.bfloat16
I32 = mybir.dt.int32
U32 = mybir.dt.uint32
U8 = mybir.dt.uint8
FP8X4 = mybir.dt.float8_e4m3fn_x4
ADD = mybir.AluOpType.add
MULT = mybir.AluOpType.mult
SIGMOID = mybir.ActivationFunctionType.Sigmoid

P = 128
K_PASS = 512
BATCH = 256
M_TILES = BATCH // P
D_IN = 16384
D_H = 1024
N_TILE = 512
N_TILES = D_H // N_TILE
ROUND = 4
X_ROUNDS = D_IN // (ROUND * K_PASS)
ROUNDS = 1 + X_ROUNDS
W_LOAD = 2
SCALE_ROWS = K_PASS // 32
RATIO_COLS = M_TILES * D_H // X_ROUNDS
AHEAD = 3

FLOPS = 2 * BATCH * (D_IN + D_H) * D_H


def groups_in(r):
    return D_H // K_PASS if r == 0 else ROUND


def weight_blocks(r):
    if r < ROUNDS - 1:
        return [(g, W_LOAD, 0, N_TILES) for g in range(0, groups_in(r), W_LOAD)]
    early = [(0, ROUND, j, 1) for j in range(N_TILES - 1)]
    return early + [(g, W_LOAD, N_TILES - 1, 1) for g in range(0, ROUND, W_LOAD)]


def tile_slstmcell_pb_k_kernel(
    tc, x, h_prev, c, n, W_o_words, W_o_scales, b_o, U_o_words, U_o_scales, out
):
    nc = tc.nc

    x_rows = x.rearrange("(p m) k -> p m k", m=M_TILES)
    h_rows = h_prev.rearrange("(p m) k -> p m k", m=M_TILES)
    c_rows = c.rearrange("(p m) j -> p (m j)", m=M_TILES)
    n_rows = n.rearrange("(p m) j -> p (m j)", m=M_TILES)
    out_rows = out.rearrange("(p m) j -> p m j", m=M_TILES)
    w_words = W_o_words.rearrange("g p j t -> p g (j t)").bitcast(I32)
    u_words = U_o_words.rearrange("g p j t -> p g (j t)").bitcast(I32)
    w_scale_rows = W_o_scales.bitcast(I32).rearrange("(r i) q w -> q i r w", i=ROUND)
    u_scale_rows = U_o_scales.bitcast(I32)

    with ExitStack() as ctx:
        keep = ctx.enter_context(tc.tile_pool(name="keep", bufs=1))
        act_pool = ctx.enter_context(tc.tile_pool(name="act", bufs=AHEAD + 2))
        w_pool = ctx.enter_context(tc.tile_pool(name="w", bufs=(AHEAD + 1) * ROUND // W_LOAD + 1))
        sorted_pool = ctx.enter_context(tc.tile_pool(name="sorted", bufs=2))
        grouped_pool = ctx.enter_context(tc.tile_pool(name="grouped", bufs=4))
        code_pool = ctx.enter_context(tc.tile_pool(name="codes", bufs=3))
        work = ctx.enter_context(tc.tile_pool(name="work", bufs=2))
        readout = ctx.enter_context(tc.tile_pool(name="readout", bufs=M_TILES * N_TILES))
        sums = ctx.enter_context(tc.psum_pool(name="sums", bufs=1))
        banks = ctx.enter_context(tc.psum_pool(name="banks", bufs=ROUND))
        ctx.enter_context(tc.manual_schedule())

        planes = keep.tile([P, ROUNDS, D_H], U8, align_bytes=64)
        planes_i32 = planes[:].bitcast(I32)
        nc.vector.memset(planes_i32, 0)
        bias_row = keep.tile([P, D_H], BF16)
        nc.vector.memset(bias_row[:].bitcast(I32), 0)
        ones = keep.tile([P, P], BF16)
        nc.vector.memset(ones[:], 1.0)
        table_in = keep.tile([P, 1], F32)
        nc.vector.memset(table_in[:], 0.0)
        ident = keep.tile([P, P], F32)
        make_identity(nc, ident[:])
        table_out = keep.tile([P, 1], F32)
        nc.scalar.activation(out=table_out[:], in_=table_in[:], func=SIGMOID)

        acts = {}
        weights = {}
        c_sb = keep.tile([P, M_TILES * D_H], BF16)

        def load_activations(r):
            cols = groups_in(r) * K_PASS
            act = act_pool.tile([P, M_TILES, cols], BF16, name="act")
            if r == 0:
                nc.sync.dma_start(out=act[:], in_=h_rows)
            else:
                nc.sync.dma_start(out=act[:], in_=x_rows[:, :, (r - 1) * cols : r * cols])
            acts[r] = act

        def load_weights(r):
            src = u_words if r == 0 else w_words[:, (r - 1) * ROUND : r * ROUND, :]
            for block in weight_blocks(r):
                g0, n_groups, j0, n_tiles = block
                words = w_pool.tile(
                    [P, n_groups, n_tiles * N_TILE], U32, name="words", align_bytes=64
                )
                nc.sync.dma_start(
                    out=words[:].bitcast(I32),
                    in_=src[:, g0 : g0 + n_groups, j0 * N_TILE : (j0 + n_tiles) * N_TILE],
                )
                weights[(r, block)] = words
                if r == ROUNDS - 2 and block == weight_blocks(r)[0]:
                    nc.sync.dma_start(out=c_sb[:], in_=c_rows)

        def load_scale_rows():
            for quad in range(SCALE_ROWS // 4):
                nc.sync.dma_start(
                    out=planes_i32[32 * quad : 32 * quad + 8, 0, :],
                    in_=u_scale_rows[:, 4 * quad : 4 * quad + 4, :],
                )
            for q in range(SCALE_ROWS):
                first = 32 * (q // 4) + q % 4
                nc.sync.dma_start(
                    out=planes_i32[first : first + 4 * ROUND : 4, 1:ROUNDS, :],
                    in_=w_scale_rows[q],
                )

        load_activations(0)
        load_activations(1)
        nc.sync.dma_start(out=bias_row[0:1, :], in_=b_o.unsqueeze(0))
        load_scale_rows()
        load_activations(2)
        load_weights(0)
        load_activations(3)
        load_weights(1)
        n_sb = keep.tile([P, M_TILES * D_H], BF16)
        nc.sync.dma_start(out=n_sb[:], in_=n_rows)
        load_activations(4)
        load_weights(2)

        acc = {}
        for m in range(M_TILES):
            for j in range(N_TILES):
                acc[(m, j)] = sums.tile([P, N_TILE], F32, name="acc%d%d" % (m, j))
        bias_all = keep.tile([P, D_H], F32)
        inv_all = keep.tile([P, M_TILES * D_H], F32)
        ratio = keep.tile([P, M_TILES * D_H], F32)
        codes = {}
        sorted_pairs = {}

        def sort_pairs(r):
            pairs = sorted_pool.tile([P, M_TILES, ROUND, 2, P], F32, name="pairs")
            for m in range(M_TILES):
                nc.scalar.copy(
                    out=pairs[:, m, 0 : groups_in(r), :, :],
                    in_=acts[r][:, m, :].bitcast(F32).rearrange("p (g q u) -> p g u q", q=P, u=2),
                )
            sorted_pairs[r] = pairs

        def transpose_and_quantise(r):
            x_words = code_pool.tile([P, ROUND, BATCH], U32, name="x_words", align_bytes=64)
            x_planes = code_pool.tile([P, ROUND, BATCH], U8, name="x_planes", align_bytes=64)
            codes[r] = (x_words, x_planes)
            for g in range(groups_in(r)):
                bank = banks.tile([P, 2, BATCH], F32, name="bank")
                for u in range(2):
                    for m in range(M_TILES):
                        nc.tensor.transpose(
                            bank[:, u, m * P : (m + 1) * P], sorted_pairs[r][:, m, g, u, :], ident[:]
                        )
                grouped = grouped_pool.tile([P, BATCH * 4], BF16, name="grouped", align_bytes=64)
                nc.scalar.copy(
                    out=grouped[:].bitcast(F32).rearrange("p (b u) -> p b u", u=2),
                    in_=bank[:].rearrange("p u b -> p b u"),
                )
                nc.vector.quantize_mx(
                    out=x_words[:, g, :].bitcast(FP8X4), scales=x_planes[:, g, :], in_=grouped[:]
                )

        def inverse_block(i):
            cols = slice(i * RATIO_COLS, (i + 1) * RATIO_COLS)
            den = work.tile([P, RATIO_COLS], F32, name="den")
            nc.vector.tensor_scalar(
                out=den[:], in0=n_sb[:, cols], scalar1=1e-6, scalar2=None, op0=ADD
            )
            nc.vector.reciprocal(out=inv_all[:, cols], in_=den[:])

        def ratios():
            for j in range(N_TILES):
                for m in range(M_TILES):
                    cols = slice(m * D_H + j * N_TILE, m * D_H + (j + 1) * N_TILE)
                    nc.vector.tensor_tensor(
                        out=ratio[:, cols], in0=inv_all[:, cols], in1=c_sb[:, cols], op=MULT
                    )

        def spread_bias():
            for j in range(N_TILES):
                cols = slice(j * N_TILE, (j + 1) * N_TILE)
                bank = banks.tile([P, N_TILE], F32, name="bank")
                nc.tensor.matmul(
                    out=bank[:], lhsT=ones[:], rhs=bias_row[:, cols], start=True, stop=True
                )
                nc.scalar.copy(out=bias_all[:, cols], in_=bank[:])

        def passes(r, block):
            x_words, x_planes = codes[r]
            g0, n_groups, j0, n_tiles = block
            words = weights[(r, block)]
            for m in range(M_TILES):
                rows = slice(m * P, (m + 1) * P)
                for g in range(g0, g0 + n_groups):
                    for j in range(j0, j0 + n_tiles):
                        nc.tensor.matmul_mx(
                            out=acc[(m, j)][:],
                            lhsT=x_words[:, g, rows].bitcast(FP8X4),
                            lhsT_scale=x_planes[:, g, rows],
                            rhs=words[:, g - g0, (j - j0) * N_TILE : (j - j0 + 1) * N_TILE].bitcast(
                                FP8X4
                            ),
                            rhs_scale=planes[4 * g : P, r, j * N_TILE : (j + 1) * N_TILE],
                            start=(r == 0 and g == 0),
                            stop=(r == ROUNDS - 1 and g == ROUND - 1),
                        )

        def read_out(j):
            gates = []
            for m in range(M_TILES):
                pre = readout.tile([P, N_TILE], F32, name="pre")
                nc.vector.tensor_tensor(
                    out=pre[:],
                    in0=acc[(m, j)][:],
                    in1=bias_all[:, j * N_TILE : (j + 1) * N_TILE],
                    op=ADD,
                )
                gate = readout.tile([P, N_TILE], F32, name="gate")
                nc.scalar.activation(out=gate[:], in_=pre[:], func=SIGMOID)
                gates.append(gate)
            for m in range(M_TILES):
                res = readout.tile([P, N_TILE], F32, name="res")
                nc.vector.tensor_tensor(
                    out=res[:],
                    in0=gates[m][:],
                    in1=ratio[:, m * D_H + j * N_TILE : m * D_H + (j + 1) * N_TILE],
                    op=MULT,
                )
                nc.sync.dma_start(out=out_rows[:, m, j * N_TILE : (j + 1) * N_TILE], in_=res[:])

        sort_pairs(0)
        sort_pairs(1)
        transpose_and_quantise(0)
        for r in range(ROUNDS):
            if r + AHEAD + 2 < ROUNDS:
                load_activations(r + AHEAD + 2)
            if r + AHEAD < ROUNDS:
                load_weights(r + AHEAD)
            if r + 1 < ROUNDS:
                transpose_and_quantise(r + 1)
                inverse_block(r)
            if r == ROUNDS - 2:
                ratios()
            if r + 2 < ROUNDS:
                sort_pairs(r + 2)
            if r == 0:
                spread_bias()
            for block in weight_blocks(r):
                passes(r, block)
                g0, n_groups, j0, n_tiles = block
                if r == ROUNDS - 1 and g0 + n_groups == ROUND:
                    read_out(j0)
